import numpy as np
import ml_dtypes


def mxq(x, axis, fmt="e4m3"):
    dtype, down = {"e4m3": (ml_dtypes.float8_e4m3fn, 7), "e5m2": (ml_dtypes.float8_e5m2, 14)}[fmt]
    v = np.moveaxis(np.asarray(x, np.float32).astype(ml_dtypes.bfloat16).astype(np.float64), axis, -1)
    blocks = v.reshape(v.shape[:-1] + (-1, 32))
    amax = np.abs(blocks).max(-1, keepdims=True)
    byte = np.maximum(np.where(amax > 0, np.frexp(amax)[1] - 1 + 127, 0) - down, 1)
    scale = np.exp2(byte - 127.0)
    codes = (blocks / scale).astype(np.float32).astype(dtype).astype(np.float64)
    return np.moveaxis((codes * scale).reshape(v.shape), -1, axis)


WIDE = False


def mx_kscale(k):
    if not WIDE:
        return np.ones(k)
    levels = np.array([10, -10, 5, -5, 0])
    a = np.random.permutation(np.resize(levels, k // 512 * 4)).reshape(k // 512, 4)
    idx = np.arange(k)
    return np.exp2(a[idx // 512, idx % 128 // 32])


BF16 = ml_dtypes.bfloat16


def bf(x):
    return np.asarray(x, np.float32).astype(BF16)


def f64(x):
    return np.asarray(x).astype(np.float64)


B, T, H, HK, D, C = 8, 512, 4, 1, 256, 512
G = H // HK
CLIP = 100.0
QS, KN, KB, VB = 9.0, 0.2, 9.0, 0.4


def setup_inputs():
    s = mx_kscale(C)
    kb = np.random.standard_normal(HK * D) * KB
    return {"x": bf(np.random.standard_normal((B, T, C)) * s),
            "Wv": bf(np.random.standard_normal((C, HK * D)) / np.sqrt(C) / s[:, None]),
            "bv": bf(np.random.standard_normal(HK * D) * VB),
            "q": bf(np.random.standard_normal((B, T, H * D)) * QS),
            "k": bf(np.random.standard_normal((B, T, HK * D)) * KN + kb)}


def reference(x, Wv, bv, q, k):
    v = (mxq(f64(x).reshape(B * T, C), 1, "e4m3") @ mxq(f64(Wv), 0, "e4m3")) + f64(bv)
    vh = v.reshape(B, T, HK, D).transpose(0, 2, 1, 3)
    qh = f64(q).reshape(B, T, HK, G, D).transpose(0, 2, 3, 1, 4).reshape(B, HK, G * T, D)
    kh = f64(k).reshape(B, T, HK, D).transpose(0, 2, 3, 1)
    s = np.clip(qh @ kh * (1.0 / np.sqrt(D)), -CLIP, CLIP)
    e = np.exp(s - s.max(-1, keepdims=True))
    o = (mxq(e, 3, "e4m3") @ mxq(vh, 2, "e4m3")) / e.sum(-1, keepdims=True)
    return o.reshape(B, HK, G, T, D).transpose(0, 3, 1, 2, 4).reshape(B, T, H * D)

@@ -1,0 +1,296 @@
+from contextlib import ExitStack
+
+import concourse.mybir as mybir
+from concourse.masks import make_identity
+
+F32 = mybir.dt.float32
+BF16 = mybir.dt.bfloat16
+U32 = mybir.dt.uint32
+U8 = mybir.dt.uint8
+FP8X4 = mybir.dt.float8_e4m3fn_x4
+ALU = mybir.AluOpType
+ACT = mybir.ActivationFunctionType
+
+B, T, H, D, C = 8, 512, 4, 256, 512
+P = 128
+PACK = 4
+TILES = T // P
+GROUPS = B * TILES
+BANK = 512
+SCALE = 1.0 / 16.0
+CLIP_RAW = 100.0 * 16.0
+
+FLOPS = 2 * B * T * C * D + 2 * 2 * B * H * T * T * D
+
+
+def tile_multiqueryattention_pa_t_kernel(tc, x, Wv, bv, q, k, out):
+    nc = tc.nc
+    with ExitStack() as ctx:
+        const = ctx.enter_context(tc.tile_pool(name="const", bufs=1))
+        loads = ctx.enter_context(tc.tile_pool(name="loads", bufs=2))
+        batch = ctx.enter_context(tc.tile_pool(name="batch", bufs=2))
+        work = ctx.enter_context(tc.tile_pool(name="work", bufs=3))
+        small = ctx.enter_context(tc.tile_pool(name="small", bufs=4))
+        ps_s = ctx.enter_context(tc.psum_pool(name="ps_s", bufs=3))
+        ps_a = ctx.enter_context(tc.psum_pool(name="ps_a", bufs=3))
+        ps_p = ctx.enter_context(tc.psum_pool(name="ps_p", bufs=2))
+        ctx.enter_context(tc.manual_schedule())
+
+        ident = const.tile([P, P], F32)
+        make_identity(nc, ident[:])
+
+        def transpose_words(bank, rows_bf16):
+            words = rows_bf16.bitcast(F32)
+            for i in range(BANK // P):
+                nc.tensor.transpose(bank[:, i * P : (i + 1) * P], words[:, i * P : (i + 1) * P], ident[:])
+
+        w_raw = const.tile([P, PACK, D], BF16)
+        bias = const.tile([P, D], BF16)
+        w_grouped = const.tile([P, D, PACK], BF16, align_bytes=64)
+        w_codes = const.tile([P, D], U32, align_bytes=64)
+        w_scales = const.tile([P, D], U8, align_bytes=64)
+
+        k_sb, q_sb, x_sb = {}, {}, {}
+        kT, x_grouped, x_mx, v_grouped, v_mx = {}, {}, {}, {}, {}
+        qT, s_ps, clipped, top, shift, e_sb, rowsum = {}, {}, {}, {}, {}, {}, {}
+        eT_ps, e_grouped, e_mx, inverse, o_ps, o_sb = {}, {}, {}, {}, {}, {}
+
+        def load_batch(b):
+            k_sb[b] = loads.tile([P, TILES * D], BF16, name="k_sb")
+            nc.sync.dma_start(
+                out=k_sb[b][:].rearrange("p (a d) -> p a d", a=TILES),
+                in_=k[b].rearrange("(a p) d -> p a d", p=P),
+            )
+            q_sb[b] = loads.tile([P, TILES * H * D], BF16, name="q_sb")
+            nc.sync.dma_start(out=q_sb[b][:], in_=q[b].rearrange("(p t) f -> p (t f)", t=TILES))
+            x_sb[b] = loads.tile([P, TILES * C], BF16, name="x_sb")
+            nc.sync.dma_start(
+                out=x_sb[b][:].rearrange("p (u f) -> p u f", u=2),
+                in_=x[b].rearrange("(u p e) c -> p u (e c)", u=2, p=P, e=2),
+            )
+
+        def keys_T(b):
+            bank = ps_p.tile([P, BANK], F32, name="bank", tag="prep")
+            transpose_words(bank, k_sb[b][:])
+            kT[b] = batch.tile([P, T * 2], BF16, name="kT")
+            nc.vector.tensor_copy(out=kT[b][:].bitcast(F32), in_=bank[:])
+
+        def queries_T(j):
+            b, t = divmod(j, TILES)
+            bank = ps_p.tile([P, BANK], F32, name="bank", tag="prep")
+            transpose_words(bank, q_sb[b][:, t * H * D : (t + 1) * H * D])
+            qT[j] = work.tile([P, H * P * 2], BF16, name="qT")
+            nc.scalar.copy(out=qT[j][:].bitcast(F32), in_=bank[:])
+
+        def x_T(b, half):
+            if half == 0:
+                x_grouped[b] = batch.tile([P, T * PACK], BF16, name="x_grouped", align_bytes=64)
+            bank = ps_p.tile([P, BANK], F32, name="bank", tag="prep")
+            transpose_words(bank, x_sb[b][:, half * 2 * C : (half + 1) * 2 * C])
+            nc.vector.tensor_copy(
+                out=x_grouped[b][:, half * 2 * BANK : (half + 1) * 2 * BANK]
+                .bitcast(F32)
+                .rearrange("p (a r u) -> p a r u", a=2, u=2),
+                in_=bank[:].rearrange("p (a u r) -> p a r u", a=2, u=2),
+            )
+            if half == 1:
+                codes = batch.tile([P, T], U32, name="x_codes", align_bytes=64)
+                scales = batch.tile([P, T], U8, name="x_scales", align_bytes=64)
+                nc.vector.quantize_mx(out=codes[:].bitcast(FP8X4), scales=scales[:], in_=x_grouped[b][:])
+                x_mx[b] = (codes, scales)
+
+        def values(b, half):
+            if half == 0:
+                v_grouped[b] = batch.tile([P, D, PACK], BF16, name="v_grouped", align_bytes=64)
+            d_cols = slice(half * P, (half + 1) * P)
+            codes, scales = x_mx[b]
+            bank = ps_p.tile([P, BANK], F32, name="bank", tag="prep")
+            for a in range(TILES):
+                rows = slice(a * P, (a + 1) * P)
+                nc.tensor.matmul_mx(
+                    out=bank[:, rows],
+                    lhsT=codes[:, rows].bitcast(FP8X4),
+                    lhsT_scale=scales[:, rows],
+                    rhs=w_codes[:, d_cols].bitcast(FP8X4),
+                    rhs_scale=w_scales[:, d_cols],
+                    start=True,
+                    stop=True,
+                )
+            nc.vector.tensor_tensor(
+                out=v_grouped[b][:, d_cols, :],
+                in0=bank[:].rearrange("p (a d) -> p d a", a=TILES),
+                in1=bias[:, d_cols].unsqueeze(2).to_broadcast([P, P, PACK]),
+                op=ALU.add,
+            )
+            if half == 1:
+                v_codes = batch.tile([P, D], U32, name="v_codes", align_bytes=64)
+                v_scales = batch.tile([P, D], U8, name="v_scales", align_bytes=64)
+                nc.vector.quantize_mx(
+                    out=v_codes[:].bitcast(FP8X4),
+                    scales=v_scales[:],
+                    in_=v_grouped[b][:].rearrange("p d a -> p (d a)"),
+                )
+                v_mx[b] = (v_codes, v_scales)
+
+        def scores(j, h):
+            q_view = qT[j][:].rearrange("p (h r e) -> p h r e", h=H, e=2)
+            k_view = kT[j // TILES][:].rearrange("p (r e) -> p r e", e=2)
+            s_ps[j, h] = ps_s.tile([P, T], F32, name="s_ps")
+            for e in range(2):
+                nc.tensor.matmul(
+                    out=s_ps[j, h][:], lhsT=q_view[:, h, :, e], rhs=k_view[:, :, e], start=(e == 0), stop=(e == 1)
+                )
+
+        def clip_and_max(j, h):
+            if h == 0:
+                clipped[j] = work.tile([P, H, T], F32, name="clipped")
+                top[j] = small.tile([P, H], F32, name="top")
+            nc.vector.tensor_scalar(
+                out=clipped[j][:, h, :],
+                in0=s_ps[j, h][:],
+                scalar1=CLIP_RAW,
+                scalar2=-CLIP_RAW,
+                op0=ALU.min,
+                op1=ALU.max,
+                accum_out=top[j][:, h : h + 1],
+            )
+
+        def finish_clip(j):
+            nc.vector.tensor_scalar_max(out=clipped[j][:], in0=clipped[j][:], scalar1=-CLIP_RAW)
+            shift[j] = small.tile([P, H], F32, name="shift")
+            nc.vector.tensor_scalar_mul(out=shift[j][:], in0=top[j][:], scalar1=-SCALE)
+
+        def exponentials(j):
+            e_sb[j] = work.tile([P, H * T], BF16, name="e_sb")
+            rowsum[j] = small.tile([P, H], F32, name="rowsum")
+            for h in range(H):
+                nc.scalar.activation(
+                    out=e_sb[j][:, h * T : (h + 1) * T],
+                    in_=clipped[j][:, h, :],
+                    func=ACT.Exp,
+                    bias=shift[j][:, h : h + 1],
+                    scale=SCALE,
+                    accum_out=rowsum[j][:, h : h + 1],
+                )
+
+        def e_T(j, pair):
+            eT_ps[j, pair] = ps_a.tile([P, BANK], F32, name="eT_ps", tag="after")
+            transpose_words(eT_ps[j, pair], e_sb[j][:, pair * 2 * T : (pair + 1) * 2 * T])
+
+        def e_out(j, pair):
+            if pair == 0:
+                e_grouped[j] = work.tile([P, H * P * PACK], BF16, name="e_grouped", align_bytes=64)
+            nc.scalar.copy(
+                out=e_grouped[j][:, pair * 2 * BANK : (pair + 1) * 2 * BANK]
+                .bitcast(F32)
+                .rearrange("p (h r u) -> p h r u", h=2, u=2),
+                in_=eT_ps[j, pair][:].rearrange("p (h u r) -> p h r u", h=2, u=2),
+            )
+
+        def quantise_e(j):
+            codes = work.tile([P, H * P], U32, name="e_codes", align_bytes=64)
+            scales = work.tile([P, H * P], U8, name="e_scales", align_bytes=64)
+            nc.vector.quantize_mx(out=codes[:].bitcast(FP8X4), scales=scales[:], in_=e_grouped[j][:])
+            e_mx[j] = (codes, scales)
+            inverse[j] = small.tile([P, H], F32, name="inverse")
+            nc.vector.reciprocal(out=inverse[j][:], in_=rowsum[j][:])
+
+        def weighted_values(j):
+            codes, scales = e_mx[j]
+            v_codes, v_scales = v_mx[j // TILES]
+            for h in range(H):
+                if h % 2 == 0:
+                    o_ps[j, h // 2] = ps_a.tile([P, BANK], F32, name="o_ps", tag="after")
+                rows = slice(h * P, (h + 1) * P)
+                nc.tensor.matmul_mx(
+                    out=o_ps[j, h // 2][:, (h % 2) * D : (h % 2 + 1) * D],
+                    lhsT=codes[:, rows].bitcast(FP8X4),
+                    lhsT_scale=scales[:, rows],
+                    rhs=v_codes[:].bitcast(FP8X4),
+                    rhs_scale=v_scales[:],
+                    start=True,
+                    stop=True,
+                )
+
+        def normalise(j, pair):
+            if pair == 0:
+                o_sb[j] = work.tile([P, H * D], F32, name="o_sb")
+            for i in range(2):
+                h = 2 * pair + i
+                nc.scalar.activation(
+                    out=o_sb[j][:, h * D : (h + 1) * D],
+                    in_=o_ps[j, pair][:, i * D : (i + 1) * D],
+                    func=ACT.Copy,
+                    scale=inverse[j][:, h : h + 1],
+                )
+
+        def store(j):
+            b, t = divmod(j, TILES)
+            nc.sync.dma_start(out=out[b].rearrange("(p t) f -> p t f", t=TILES)[:, t, :], in_=o_sb[j][:])
+
+        load_batch(0)
+        nc.sync.dma_start(
+            out=w_raw[:].rearrange("p (u e) d -> p u (e d)", u=2),
+            in_=Wv.rearrange("(u p e) d -> p u (e d)", u=2, p=P, e=2),
+        )
+        nc.sync.dma_start(out=bias[:], in_=bv.partition_broadcast(P))
+        load_batch(1)
+        keys_T(0)
+        queries_T(0)
+        queries_T(1)
+        for h in range(H - 1):
+            scores(0, h)
+
+        for j in range(GROUPS + 2):
+            b, t = divmod(j, TILES)
+            clipping, exponentiating, finishing = j < GROUPS, 1 <= j <= GROUPS, j >= 2
+            if finishing:
+                quantise_e(j - 2)
+            if exponentiating:
+                exponentials(j - 1)
+                e_T(j - 1, 0)
+            if finishing:
+                weighted_values(j - 2)
+            if clipping:
+                clip_and_max(j, 0)
+                scores(j, H - 1)
+                for h in range(1, H):
+                    clip_and_max(j, h)
+            if exponentiating:
+                e_out(j - 1, 0)
+            if finishing:
+                normalise(j - 2, 0)
+            if j + 2 < GROUPS:
+                queries_T(j + 2)
+            if exponentiating:
+                e_T(j - 1, 1)
+                e_out(j - 1, 1)
+            if finishing:
+                normalise(j - 2, 1)
+                store(j - 2)
+            if clipping:
+                finish_clip(j)
+                if j == 0:
+                    nc.vector.tensor_copy(out=w_grouped[:], in_=w_raw[:].rearrange("p t d -> p d t"))
+                    x_T(0, 0)
+                    nc.vector.quantize_mx(
+                        out=w_codes[:].bitcast(FP8X4),
+                        scales=w_scales[:],
+                        in_=w_grouped[:].rearrange("p d t -> p (d t)"),
+                    )
+                    x_T(0, 1)
+                if t == 0:
+                    values(b, 0)
+                if t == 1:
+                    values(b, 1)
+                if t == 1 and b + 1 < B:
+                    keys_T(b + 1)
+                if t == 2 and b + 1 < B:
+                    x_T(b + 1, 0)
+                if t == 2 and b + 2 < B:
+                    load_batch(b + 2)
+                if t == 3 and b + 1 < B:
+                    x_T(b + 1, 1)
+            if j + 1 < GROUPS:
+                for h in range(H - 1):
+                    scores(j + 1, h)

@@ -51,7 +51,7 @@ def tile_multiqueryattention_pa_t_kernel(tc, x, Wv, bv, q, k, out):
         w_scales = const.tile([P, D], U8, align_bytes=64)
 
         k_sb, q_sb, x_sb = {}, {}, {}
-        kT, x_grouped, x_mx, v_grouped, v_mx = {}, {}, {}, {}, {}
+        kT, x_grouped, x_mx, v_ps, v_grouped, v_mx = {}, {}, {}, {}, {}, {}
         qT, s_ps, clipped, top, shift, e_sb, rowsum = {}, {}, {}, {}, {}, {}, {}
         eT_ps, e_grouped, e_mx, inverse, o_ps, o_sb = {}, {}, {}, {}, {}, {}
 
@@ -80,7 +80,7 @@ def tile_multiqueryattention_pa_t_kernel(tc, x, Wv, bv, q, k, out):
             bank = ps_p.tile([P, BANK], F32, name="bank", tag="prep")
             transpose_words(bank, q_sb[b][:, t * H * D : (t + 1) * H * D])
             qT[j] = work.tile([P, H * P * 2], BF16, name="qT")
-            nc.scalar.copy(out=qT[j][:].bitcast(F32), in_=bank[:])
+            nc.vector.tensor_copy(out=qT[j][:].bitcast(F32), in_=bank[:])
 
         def x_T(b, half):
             if half == 0:
@@ -99,16 +99,14 @@ def tile_multiqueryattention_pa_t_kernel(tc, x, Wv, bv, q, k, out):
                 nc.vector.quantize_mx(out=codes[:].bitcast(FP8X4), scales=scales[:], in_=x_grouped[b][:])
                 x_mx[b] = (codes, scales)
 
-        def values(b, half):
-            if half == 0:
-                v_grouped[b] = batch.tile([P, D, PACK], BF16, name="v_grouped", align_bytes=64)
+        def project_values(b, half):
             d_cols = slice(half * P, (half + 1) * P)
             codes, scales = x_mx[b]
-            bank = ps_p.tile([P, BANK], F32, name="bank", tag="prep")
+            v_ps[b, half] = ps_p.tile([P, BANK], F32, name="v_ps", tag="prep")
             for a in range(TILES):
                 rows = slice(a * P, (a + 1) * P)
                 nc.tensor.matmul_mx(
-                    out=bank[:, rows],
+                    out=v_ps[b, half][:, rows],
                     lhsT=codes[:, rows].bitcast(FP8X4),
                     lhsT_scale=scales[:, rows],
                     rhs=w_codes[:, d_cols].bitcast(FP8X4),
@@ -116,9 +114,14 @@ def tile_multiqueryattention_pa_t_kernel(tc, x, Wv, bv, q, k, out):
                     start=True,
                     stop=True,
                 )
+
+        def finish_values(b, half):
+            if half == 0:
+                v_grouped[b] = batch.tile([P, D, PACK], BF16, name="v_grouped", align_bytes=64)
+            d_cols = slice(half * P, (half + 1) * P)
             nc.vector.tensor_tensor(
                 out=v_grouped[b][:, d_cols, :],
-                in0=bank[:].rearrange("p (a d) -> p d a", a=TILES),
+                in0=v_ps[b, half][:].rearrange("p (a d) -> p d a", a=TILES),
                 in1=bias[:, d_cols].unsqueeze(2).to_broadcast([P, P, PACK]),
                 op=ALU.add,
             )
@@ -155,8 +158,17 @@ def tile_multiqueryattention_pa_t_kernel(tc, x, Wv, bv, q, k, out):
                 accum_out=top[j][:, h : h + 1],
             )
 
-        def finish_clip(j):
-            nc.vector.tensor_scalar_max(out=clipped[j][:], in0=clipped[j][:], scalar1=-CLIP_RAW)
+        def lower_clip(j, h):
+            nc.gpsimd.tensor_scalar(
+                out=clipped[j][:, h, :],
+                in0=clipped[j][:, h, :],
+                scalar1=CLIP_RAW,
+                scalar2=-CLIP_RAW,
+                op0=ALU.min,
+                op1=ALU.max,
+            )
+
+        def make_shift(j):
             shift[j] = small.tile([P, H], F32, name="shift")
             nc.vector.tensor_scalar_mul(out=shift[j][:], in0=top[j][:], scalar1=-SCALE)
 
@@ -244,53 +256,57 @@ def tile_multiqueryattention_pa_t_kernel(tc, x, Wv, bv, q, k, out):
         for j in range(GROUPS + 2):
             b, t = divmod(j, TILES)
             clipping, exponentiating, finishing = j < GROUPS, 1 <= j <= GROUPS, j >= 2
+            projecting = clipping and t < 2 and b > 0
             if finishing:
                 quantise_e(j - 2)
+                weighted_values(j - 2)
+            if projecting:
+                project_values(b, t)
             if exponentiating:
                 exponentials(j - 1)
-                e_T(j - 1, 0)
-            if finishing:
-                weighted_values(j - 2)
             if clipping:
                 clip_and_max(j, 0)
+                lower_clip(j, 0)
                 scores(j, H - 1)
                 for h in range(1, H):
                     clip_and_max(j, h)
-            if exponentiating:
-                e_out(j - 1, 0)
+                    lower_clip(j, h)
+                make_shift(j)
             if finishing:
                 normalise(j - 2, 0)
-            if j + 2 < GROUPS:
-                queries_T(j + 2)
-            if exponentiating:
-                e_T(j - 1, 1)
-                e_out(j - 1, 1)
-            if finishing:
                 normalise(j - 2, 1)
                 store(j - 2)
-            if clipping:
-                finish_clip(j)
-                if j == 0:
-                    nc.vector.tensor_copy(out=w_grouped[:], in_=w_raw[:].rearrange("p t d -> p d t"))
-                    x_T(0, 0)
-                    nc.vector.quantize_mx(
-                        out=w_codes[:].bitcast(FP8X4),
-                        scales=w_scales[:],
-                        in_=w_grouped[:].rearrange("p d t -> p (d t)"),
-                    )
-                    x_T(0, 1)
-                if t == 0:
-                    values(b, 0)
-                if t == 1:
-                    values(b, 1)
-                if t == 1 and b + 1 < B:
-                    keys_T(b + 1)
-                if t == 2 and b + 1 < B:
-                    x_T(b + 1, 0)
-                if t == 2 and b + 2 < B:
-                    load_batch(b + 2)
-                if t == 3 and b + 1 < B:
-                    x_T(b + 1, 1)
+            if exponentiating:
+                e_T(j - 1, 0)
+                e_T(j - 1, 1)
+                e_out(j - 1, 0)
+                e_out(j - 1, 1)
+            if j + 2 < GROUPS:
+                queries_T(j + 2)
+            if projecting:
+                finish_values(b, t)
+            if j == 0:
+                nc.vector.tensor_copy(out=w_grouped[:], in_=w_raw[:].rearrange("p t d -> p d t"))
+                x_T(0, 0)
+                nc.vector.quantize_mx(
+                    out=w_codes[:].bitcast(FP8X4),
+                    scales=w_scales[:],
+                    in_=w_grouped[:].rearrange("p d t -> p (d t)"),
+                )
+                x_T(0, 1)
+            if j == 1:
+                project_values(0, 0)
+                project_values(0, 1)
+                finish_values(0, 0)
+                finish_values(0, 1)
+            if clipping and t == 1 and b + 1 < B:
+                keys_T(b + 1)
+            if clipping and t == 2 and b + 1 < B:
+                x_T(b + 1, 0)
+            if clipping and t == 2 and b + 2 < B:
+                load_batch(b + 2)
+            if clipping and t == 3 and b + 1 < B:
+                x_T(b + 1, 1)
             if j + 1 < GROUPS:
                 for h in range(H - 1):
                     scores(j + 1, h)

@@ -73,21 +73,21 @@ def tile_multiqueryattention_pa_t_kernel(tc, x, Wv, bv, q, k, out):
             bank = ps_p.tile([P, BANK], F32, name="bank", tag="prep")
             transpose_words(bank, k_sb[b][:])
             kT[b] = batch.tile([P, T * 2], BF16, name="kT")
-            nc.vector.tensor_copy(out=kT[b][:].bitcast(F32), in_=bank[:])
+            nc.scalar.copy(out=kT[b][:].bitcast(F32), in_=bank[:])
 
         def queries_T(j):
             b, t = divmod(j, TILES)
             bank = ps_p.tile([P, BANK], F32, name="bank", tag="prep")
             transpose_words(bank, q_sb[b][:, t * H * D : (t + 1) * H * D])
             qT[j] = work.tile([P, H * P * 2], BF16, name="qT")
-            nc.vector.tensor_copy(out=qT[j][:].bitcast(F32), in_=bank[:])
+            nc.scalar.copy(out=qT[j][:].bitcast(F32), in_=bank[:])
 
         def x_T(b, half):
             if half == 0:
                 x_grouped[b] = batch.tile([P, T * PACK], BF16, name="x_grouped", align_bytes=64)
             bank = ps_p.tile([P, BANK], F32, name="bank", tag="prep")
             transpose_words(bank, x_sb[b][:, half * 2 * C : (half + 1) * 2 * C])
-            nc.vector.tensor_copy(
+            nc.scalar.copy(
                 out=x_grouped[b][:, half * 2 * BANK : (half + 1) * 2 * BANK]
                 .bitcast(F32)
                 .rearrange("p (a r u) -> p a r u", a=2, u=2),
@@ -229,11 +229,10 @@ def tile_multiqueryattention_pa_t_kernel(tc, x, Wv, bv, q, k, out):
                 o_sb[j] = work.tile([P, H * D], F32, name="o_sb")
             for i in range(2):
                 h = 2 * pair + i
-                nc.scalar.activation(
+                nc.vector.tensor_scalar_mul(
                     out=o_sb[j][:, h * D : (h + 1) * D],
-                    in_=o_ps[j, pair][:, i * D : (i + 1) * D],
-                    func=ACT.Copy,
-                    scale=inverse[j][:, h : h + 1],
+                    in0=o_ps[j, pair][:, i * D : (i + 1) * D],
+                    scalar1=inverse[j][:, h : h + 1],
                 )
 
         def store(j):
@@ -268,14 +267,19 @@ def tile_multiqueryattention_pa_t_kernel(tc, x, Wv, bv, q, k, out):
                 clip_and_max(j, 0)
                 lower_clip(j, 0)
                 scores(j, H - 1)
-                for h in range(1, H):
-                    clip_and_max(j, h)
-                    lower_clip(j, h)
-                make_shift(j)
+                clip_and_max(j, 1)
+                lower_clip(j, 1)
             if finishing:
                 normalise(j - 2, 0)
                 normalise(j - 2, 1)
                 store(j - 2)
+            if projecting:
+                finish_values(b, t)
+            if clipping:
+                for h in range(2, H):
+                    clip_and_max(j, h)
+                    lower_clip(j, h)
+                make_shift(j)
             if exponentiating:
                 e_T(j - 1, 0)
                 e_T(j - 1, 1)
@@ -283,8 +287,6 @@ def tile_multiqueryattention_pa_t_kernel(tc, x, Wv, bv, q, k, out):
                 e_out(j - 1, 1)
             if j + 2 < GROUPS:
                 queries_T(j + 2)
-            if projecting:
-                finish_values(b, t)
             if j == 0:
                 nc.vector.tensor_copy(out=w_grouped[:], in_=w_raw[:].rearrange("p t d -> p d t"))
                 x_T(0, 0)
@@ -299,14 +301,12 @@ def tile_multiqueryattention_pa_t_kernel(tc, x, Wv, bv, q, k, out):
                 project_values(0, 1)
                 finish_values(0, 0)
                 finish_values(0, 1)
-            if clipping and t == 1 and b + 1 < B:
-                keys_T(b + 1)
+            if clipping and t < 2 and b + 1 < B:
+                x_T(b + 1, t)
             if clipping and t == 2 and b + 1 < B:
-                x_T(b + 1, 0)
+                keys_T(b + 1)
             if clipping and t == 2 and b + 2 < B:
                 load_batch(b + 2)
-            if clipping and t == 3 and b + 1 < B:
-                x_T(b + 1, 1)
             if j + 1 < GROUPS:
                 for h in range(H - 1):
                     scores(j + 1, h)

@@ -17,8 +17,9 @@ PACK = 4
 TILES = T // P
 GROUPS = B * TILES
 BANK = 512
+PAD = 8
 SCALE = 1.0 / 16.0
-CLIP_RAW = 100.0 * 16.0
+CLIP = 100.0
 
 FLOPS = 2 * B * T * C * D + 2 * 2 * B * H * T * T * D
 
@@ -52,7 +53,7 @@ def tile_multiqueryattention_pa_t_kernel(tc, x, Wv, bv, q, k, out):
 
         k_sb, q_sb, x_sb = {}, {}, {}
         kT, x_grouped, x_mx, v_ps, v_grouped, v_mx = {}, {}, {}, {}, {}, {}
-        qT, s_ps, clipped, top, shift, e_sb, rowsum = {}, {}, {}, {}, {}, {}, {}
+        qT, s_ps, clipped, e_sb, rowsum = {}, {}, {}, {}, {}
         eT_ps, e_grouped, e_mx, inverse, o_ps, o_sb = {}, {}, {}, {}, {}, {}
 
         def load_batch(b):
@@ -62,7 +63,17 @@ def tile_multiqueryattention_pa_t_kernel(tc, x, Wv, bv, q, k, out):
                 in_=k[b].rearrange("(a p) d -> p a d", p=P),
             )
             q_sb[b] = loads.tile([P, TILES * H * D], BF16, name="q_sb")
-            nc.sync.dma_start(out=q_sb[b][:], in_=q[b].rearrange("(p t) f -> p (t f)", t=TILES))
+            q_view = q[b].rearrange("(p t) f -> p t f", t=TILES)
+            pieces = [slice(0, 1), slice(1, TILES)] if b == 0 else [slice(0, TILES)]
+            for tiles in pieces:
+                nc.sync.dma_start(
+                    out=q_sb[b][:].rearrange("p (t f) -> p t f", t=TILES)[:, tiles, :], in_=q_view[:, tiles, :]
+                )
+            if b == 0:
+                nc.sync.dma_start(
+                    out=w_raw[:].rearrange("p (u e) d -> p u (e d)", u=2),
+                    in_=Wv.rearrange("(u p e) d -> p u (e d)", u=2, p=P, e=2),
+                )
             x_sb[b] = loads.tile([P, TILES * C], BF16, name="x_sb")
             nc.sync.dma_start(
                 out=x_sb[b][:].rearrange("p (u f) -> p u f", u=2),
@@ -144,46 +155,41 @@ def tile_multiqueryattention_pa_t_kernel(tc, x, Wv, bv, q, k, out):
                     out=s_ps[j, h][:], lhsT=q_view[:, h, :, e], rhs=k_view[:, :, e], start=(e == 0), stop=(e == 1)
                 )
 
-        def clip_and_max(j, h):
+        def scale_and_max(j, h):
             if h == 0:
-                clipped[j] = work.tile([P, H, T], F32, name="clipped")
-                top[j] = small.tile([P, H], F32, name="top")
+                clipped[j] = work.tile([P, H, T + PAD], F32, name="clipped")
             nc.vector.tensor_scalar(
-                out=clipped[j][:, h, :],
+                out=clipped[j][:, h, :T],
                 in0=s_ps[j, h][:],
-                scalar1=CLIP_RAW,
-                scalar2=-CLIP_RAW,
-                op0=ALU.min,
-                op1=ALU.max,
-                accum_out=top[j][:, h : h + 1],
+                scalar1=-SCALE,
+                scalar2=CLIP,
+                op0=ALU.mult,
+                op1=ALU.min,
+                accum_out=clipped[j][:, h, T : T + 1],
             )
 
-        def lower_clip(j, h):
+        def clip(j, h):
             nc.gpsimd.tensor_scalar(
-                out=clipped[j][:, h, :],
-                in0=clipped[j][:, h, :],
-                scalar1=CLIP_RAW,
-                scalar2=-CLIP_RAW,
+                out=clipped[j][:, h, : T + 1],
+                in0=clipped[j][:, h, : T + 1],
+                scalar1=CLIP,
+                scalar2=-CLIP,
                 op0=ALU.min,
                 op1=ALU.max,
             )
 
-        def make_shift(j):
-            shift[j] = small.tile([P, H], F32, name="shift")
-            nc.vector.tensor_scalar_mul(out=shift[j][:], in0=top[j][:], scalar1=-SCALE)
-
-        def exponentials(j):
-            e_sb[j] = work.tile([P, H * T], BF16, name="e_sb")
-            rowsum[j] = small.tile([P, H], F32, name="rowsum")
-            for h in range(H):
-                nc.scalar.activation(
-                    out=e_sb[j][:, h * T : (h + 1) * T],
-                    in_=clipped[j][:, h, :],
-                    func=ACT.Exp,
-                    bias=shift[j][:, h : h + 1],
-                    scale=SCALE,
-                    accum_out=rowsum[j][:, h : h + 1],
-                )
+        def exponential(j, h):
+            if h == 0:
+                e_sb[j] = work.tile([P, H * T], BF16, name="e_sb")
+                rowsum[j] = small.tile([P, H], F32, name="rowsum")
+            nc.scalar.activation(
+                out=e_sb[j][:, h * T : (h + 1) * T],
+                in_=clipped[j][:, h, :T],
+                func=ACT.Exp,
+                bias=clipped[j][:, h, T : T + 1],
+                scale=-1.0,
+                accum_out=rowsum[j][:, h : h + 1],
+            )
 
         def e_T(j, pair):
             eT_ps[j, pair] = ps_a.tile([P, BANK], F32, name="eT_ps", tag="after")
@@ -204,18 +210,19 @@ def tile_multiqueryattention_pa_t_kernel(tc, x, Wv, bv, q, k, out):
             scales = work.tile([P, H * P], U8, name="e_scales", align_bytes=64)
             nc.vector.quantize_mx(out=codes[:].bitcast(FP8X4), scales=scales[:], in_=e_grouped[j][:])
             e_mx[j] = (codes, scales)
+
+        def invert(j):
             inverse[j] = small.tile([P, H], F32, name="inverse")
             nc.vector.reciprocal(out=inverse[j][:], in_=rowsum[j][:])
 
-        def weighted_values(j):
+        def weighted_values(j, pair):
             codes, scales = e_mx[j]
             v_codes, v_scales = v_mx[j // TILES]
-            for h in range(H):
-                if h % 2 == 0:
-                    o_ps[j, h // 2] = ps_a.tile([P, BANK], F32, name="o_ps", tag="after")
-                rows = slice(h * P, (h + 1) * P)
+            o_ps[j, pair] = ps_a.tile([P, BANK], F32, name="o_ps", tag="after")
+            for i in range(2):
+                rows = slice((2 * pair + i) * P, (2 * pair + i + 1) * P)
                 nc.tensor.matmul_mx(
-                    out=o_ps[j, h // 2][:, (h % 2) * D : (h % 2 + 1) * D],
+                    out=o_ps[j, pair][:, i * D : (i + 1) * D],
                     lhsT=codes[:, rows].bitcast(FP8X4),
                     lhsT_scale=scales[:, rows],
                     rhs=v_codes[:].bitcast(FP8X4),
@@ -240,53 +247,65 @@ def tile_multiqueryattention_pa_t_kernel(tc, x, Wv, bv, q, k, out):
             nc.sync.dma_start(out=out[b].rearrange("(p t) f -> p t f", t=TILES)[:, t, :], in_=o_sb[j][:])
 
         load_batch(0)
-        nc.sync.dma_start(
-            out=w_raw[:].rearrange("p (u e) d -> p u (e d)", u=2),
-            in_=Wv.rearrange("(u p e) d -> p u (e d)", u=2, p=P, e=2),
-        )
         nc.sync.dma_start(out=bias[:], in_=bv.partition_broadcast(P))
         load_batch(1)
         keys_T(0)
         queries_T(0)
-        queries_T(1)
         for h in range(H - 1):
             scores(0, h)
+        queries_T(1)
 
         for j in range(GROUPS + 2):
             b, t = divmod(j, TILES)
             clipping, exponentiating, finishing = j < GROUPS, 1 <= j <= GROUPS, j >= 2
             projecting = clipping and t < 2 and b > 0
             if finishing:
-                quantise_e(j - 2)
-                weighted_values(j - 2)
-            if projecting:
-                project_values(b, t)
+                weighted_values(j - 2, 0)
             if exponentiating:
-                exponentials(j - 1)
+                exponential(j - 1, 0)
+                exponential(j - 1, 1)
+                e_T(j - 1, 0)
+                exponential(j - 1, 2)
+                exponential(j - 1, 3)
             if clipping:
-                clip_and_max(j, 0)
-                lower_clip(j, 0)
-                scores(j, H - 1)
-                clip_and_max(j, 1)
-                lower_clip(j, 1)
+                for h in range(3):
+                    scale_and_max(j, h)
+                    clip(j, h)
             if finishing:
                 normalise(j - 2, 0)
-                normalise(j - 2, 1)
-                store(j - 2)
-            if projecting:
-                finish_values(b, t)
-            if clipping:
-                for h in range(2, H):
-                    clip_and_max(j, h)
-                    lower_clip(j, h)
-                make_shift(j)
-            if exponentiating:
-                e_T(j - 1, 0)
-                e_T(j - 1, 1)
-                e_out(j - 1, 0)
-                e_out(j - 1, 1)
+            if clipping and t == 3 and b + 1 < B:
+                keys_T(b + 1)
             if j + 2 < GROUPS:
                 queries_T(j + 2)
+            if clipping:
+                scores(j, 3)
+            if exponentiating:
+                e_out(j - 1, 0)
+                e_T(j - 1, 1)
+            if projecting:
+                project_values(b, t)
+            if clipping:
+                scale_and_max(j, 3)
+                clip(j, 3)
+            if exponentiating:
+                invert(j - 1)
+                e_out(j - 1, 1)
+            if finishing:
+                weighted_values(j - 2, 1)
+            if projecting:
+                finish_values(b, t)
+            if finishing:
+                normalise(j - 2, 1)
+                store(j - 2)
+            if exponentiating:
+                quantise_e(j - 1)
+            if clipping and 1 <= t <= 2 and b + 1 < B:
+                x_T(b + 1, t - 1)
+            if j + 1 < GROUPS:
+                for h in range(H - 1):
+                    scores(j + 1, h)
+            if clipping and t == 2 and b + 2 < B:
+                load_batch(b + 2)
             if j == 0:
                 nc.vector.tensor_copy(out=w_grouped[:], in_=w_raw[:].rearrange("p t d -> p d t"))
                 x_T(0, 0)
@@ -301,12 +320,3 @@ def tile_multiqueryattention_pa_t_kernel(tc, x, Wv, bv, q, k, out):
                 project_values(0, 1)
                 finish_values(0, 0)
                 finish_values(0, 1)
-            if clipping and t < 2 and b + 1 < B:
-                x_T(b + 1, t)
-            if clipping and t == 2 and b + 1 < B:
-                keys_T(b + 1)
-            if clipping and t == 2 and b + 2 < B:
-                load_batch(b + 2)
-            if j + 1 < GROUPS:
-                for h in range(H - 1):
-                    scores(j + 1, h)

@@ -104,11 +104,12 @@ def tile_multiqueryattention_pa_t_kernel(tc, x, Wv, bv, q, k, out):
                 .rearrange("p (a r u) -> p a r u", a=2, u=2),
                 in_=bank[:].rearrange("p (a u r) -> p a r u", a=2, u=2),
             )
-            if half == 1:
-                codes = batch.tile([P, T], U32, name="x_codes", align_bytes=64)
-                scales = batch.tile([P, T], U8, name="x_scales", align_bytes=64)
-                nc.vector.quantize_mx(out=codes[:].bitcast(FP8X4), scales=scales[:], in_=x_grouped[b][:])
-                x_mx[b] = (codes, scales)
+
+        def quantise_x(b):
+            codes = batch.tile([P, T], U32, name="x_codes", align_bytes=64)
+            scales = batch.tile([P, T], U8, name="x_scales", align_bytes=64)
+            nc.vector.quantize_mx(out=codes[:].bitcast(FP8X4), scales=scales[:], in_=x_grouped[b][:])
+            x_mx[b] = (codes, scales)
 
         def project_values(b, half):
             d_cols = slice(half * P, (half + 1) * P)
@@ -258,65 +259,72 @@ def tile_multiqueryattention_pa_t_kernel(tc, x, Wv, bv, q, k, out):
         for j in range(GROUPS + 2):
             b, t = divmod(j, TILES)
             clipping, exponentiating, finishing = j < GROUPS, 1 <= j <= GROUPS, j >= 2
-            projecting = clipping and t < 2 and b > 0
+            projecting = clipping and (t < 2 and b > 0 or j == 1)
+            half = 0 if j == 1 else t
+            if j == 0:
+                x_T(0, 0)
+            if projecting:
+                project_values(b, half)
+            if exponentiating:
+                for h in range(H):
+                    exponential(j - 1, h)
+            if clipping:
+                scale_and_max(j, 0)
+                clip(j, 0)
+            if t == 2 and b + 1 < B:
+                keys_T(b + 1)
+                x_T(b + 1, 0)
+            if clipping:
+                scale_and_max(j, 1)
+                clip(j, 1)
             if finishing:
                 weighted_values(j - 2, 0)
-            if exponentiating:
-                exponential(j - 1, 0)
-                exponential(j - 1, 1)
-                e_T(j - 1, 0)
-                exponential(j - 1, 2)
-                exponential(j - 1, 3)
-            if clipping:
-                for h in range(3):
-                    scale_and_max(j, h)
-                    clip(j, h)
-            if finishing:
-                normalise(j - 2, 0)
-            if clipping and t == 3 and b + 1 < B:
-                keys_T(b + 1)
-            if j + 2 < GROUPS:
-                queries_T(j + 2)
+                weighted_values(j - 2, 1)
             if clipping:
                 scores(j, 3)
-            if exponentiating:
-                e_out(j - 1, 0)
-                e_T(j - 1, 1)
-            if projecting:
-                project_values(b, t)
-            if clipping:
-                scale_and_max(j, 3)
-                clip(j, 3)
-            if exponentiating:
-                invert(j - 1)
-                e_out(j - 1, 1)
             if finishing:
-                weighted_values(j - 2, 1)
-            if projecting:
-                finish_values(b, t)
+                normalise(j - 2, 0)
+            if clipping:
+                for h in range(2, H):
+                    scale_and_max(j, h)
+                    clip(j, h)
+            if j == 0:
+                nc.vector.tensor_copy(out=w_grouped[:], in_=w_raw[:].rearrange("p t d -> p d t"))
+            if exponentiating:
+                e_T(j - 1, 0)
             if finishing:
                 normalise(j - 2, 1)
                 store(j - 2)
             if exponentiating:
-                quantise_e(j - 1)
-            if clipping and 1 <= t <= 2 and b + 1 < B:
-                x_T(b + 1, t - 1)
-            if j + 1 < GROUPS:
-                for h in range(H - 1):
-                    scores(j + 1, h)
-            if clipping and t == 2 and b + 2 < B:
-                load_batch(b + 2)
+                e_out(j - 1, 0)
+            if t == 2 and b + 1 < B:
+                x_T(b + 1, 1)
+                quantise_x(b + 1)
+            if exponentiating:
+                e_T(j - 1, 1)
+                invert(j - 1)
+            if projecting:
+                finish_values(b, half)
+            if exponentiating:
+                e_out(j - 1, 1)
             if j == 0:
-                nc.vector.tensor_copy(out=w_grouped[:], in_=w_raw[:].rearrange("p t d -> p d t"))
-                x_T(0, 0)
+                x_T(0, 1)
                 nc.vector.quantize_mx(
                     out=w_codes[:].bitcast(FP8X4),
                     scales=w_scales[:],
                     in_=w_grouped[:].rearrange("p d t -> p (d t)"),
                 )
-                x_T(0, 1)
+                quantise_x(0)
+            if j + 2 < GROUPS:
+                queries_T(j + 2)
             if j == 1:
-                project_values(0, 0)
                 project_values(0, 1)
-                finish_values(0, 0)
+            if j + 1 < GROUPS:
+                for h in range(H - 1):
+                    scores(j + 1, h)
+            if exponentiating:
+                quantise_e(j - 1)
+            if j == 1:
                 finish_values(0, 1)
+            if t == 2 and b + 2 < B:
+                load_batch(b + 2)

@@ -17,9 +17,8 @@ PACK = 4
 TILES = T // P
 GROUPS = B * TILES
 BANK = 512
-PAD = 8
 SCALE = 1.0 / 16.0
-CLIP = 100.0
+CLIP_RAW = 100.0 * 16.0
 
 FLOPS = 2 * B * T * C * D + 2 * 2 * B * H * T * T * D
 
@@ -53,7 +52,7 @@ def tile_multiqueryattention_pa_t_kernel(tc, x, Wv, bv, q, k, out):
 
         k_sb, q_sb, x_sb = {}, {}, {}
         kT, x_grouped, x_mx, v_ps, v_grouped, v_mx = {}, {}, {}, {}, {}, {}
-        qT, s_ps, clipped, e_sb, rowsum = {}, {}, {}, {}, {}
+        qT, s_ps, clipped, top, shift, e_sb, rowsum = {}, {}, {}, {}, {}, {}, {}
         eT_ps, e_grouped, e_mx, inverse, o_ps, o_sb = {}, {}, {}, {}, {}, {}
 
         def load_batch(b):
@@ -156,28 +155,33 @@ def tile_multiqueryattention_pa_t_kernel(tc, x, Wv, bv, q, k, out):
                     out=s_ps[j, h][:], lhsT=q_view[:, h, :, e], rhs=k_view[:, :, e], start=(e == 0), stop=(e == 1)
                 )
 
-        def scale_and_max(j, h):
+        def clip_and_max(j, h):
             if h == 0:
-                clipped[j] = work.tile([P, H, T + PAD], F32, name="clipped")
+                clipped[j] = work.tile([P, H, T], F32, name="clipped")
+                top[j] = small.tile([P, H], F32, name="top")
             nc.vector.tensor_scalar(
-                out=clipped[j][:, h, :T],
+                out=clipped[j][:, h, :],
                 in0=s_ps[j, h][:],
-                scalar1=-SCALE,
-                scalar2=CLIP,
-                op0=ALU.mult,
-                op1=ALU.min,
-                accum_out=clipped[j][:, h, T : T + 1],
+                scalar1=CLIP_RAW,
+                scalar2=-CLIP_RAW,
+                op0=ALU.min,
+                op1=ALU.max,
+                accum_out=top[j][:, h : h + 1],
             )
 
-        def clip(j, h):
+        def lower_clip(j, h):
             nc.gpsimd.tensor_scalar(
-                out=clipped[j][:, h, : T + 1],
-                in0=clipped[j][:, h, : T + 1],
-                scalar1=CLIP,
-                scalar2=-CLIP,
+                out=clipped[j][:, h, :],
+                in0=clipped[j][:, h, :],
+                scalar1=CLIP_RAW,
+                scalar2=-CLIP_RAW,
                 op0=ALU.min,
                 op1=ALU.max,
             )
+
+        def make_shift(j):
+            shift[j] = small.tile([P, H], F32, name="shift")
+            nc.vector.tensor_scalar_mul(out=shift[j][:], in0=top[j][:], scalar1=-SCALE)
 
         def exponential(j, h):
             if h == 0:
@@ -185,10 +189,10 @@ def tile_multiqueryattention_pa_t_kernel(tc, x, Wv, bv, q, k, out):
                 rowsum[j] = small.tile([P, H], F32, name="rowsum")
             nc.scalar.activation(
                 out=e_sb[j][:, h * T : (h + 1) * T],
-                in_=clipped[j][:, h, :T],
+                in_=clipped[j][:, h, :],
                 func=ACT.Exp,
-                bias=clipped[j][:, h, T : T + 1],
-                scale=-1.0,
+                bias=shift[j][:, h : h + 1],
+                scale=SCALE,
                 accum_out=rowsum[j][:, h : h + 1],
             )
 
@@ -269,14 +273,14 @@ def tile_multiqueryattention_pa_t_kernel(tc, x, Wv, bv, q, k, out):
                 for h in range(H):
                     exponential(j - 1, h)
             if clipping:
-                scale_and_max(j, 0)
-                clip(j, 0)
+                clip_and_max(j, 0)
+                lower_clip(j, 0)
             if t == 2 and b + 1 < B:
                 keys_T(b + 1)
                 x_T(b + 1, 0)
             if clipping:
-                scale_and_max(j, 1)
-                clip(j, 1)
+                clip_and_max(j, 1)
+                lower_clip(j, 1)
             if finishing:
                 weighted_values(j - 2, 0)
                 weighted_values(j - 2, 1)
@@ -286,8 +290,8 @@ def tile_multiqueryattention_pa_t_kernel(tc, x, Wv, bv, q, k, out):
                 normalise(j - 2, 0)
             if clipping:
                 for h in range(2, H):
-                    scale_and_max(j, h)
-                    clip(j, h)
+                    clip_and_max(j, h)
+                    lower_clip(j, h)
             if j == 0:
                 nc.vector.tensor_copy(out=w_grouped[:], in_=w_raw[:].rearrange("p t d -> p d t"))
             if exponentiating:
@@ -295,6 +299,8 @@ def tile_multiqueryattention_pa_t_kernel(tc, x, Wv, bv, q, k, out):
             if finishing:
                 normalise(j - 2, 1)
                 store(j - 2)
+            if clipping:
+                make_shift(j)
             if exponentiating:
                 e_out(j - 1, 0)
             if t == 2 and b + 1 < B:

@@ -18,7 +18,7 @@ TILES = T // P
 GROUPS = B * TILES
 BANK = 512
 SCALE = 1.0 / 16.0
-CLIP_RAW = 100.0 * 16.0
+CLIP = 100.0
 
 FLOPS = 2 * B * T * C * D + 2 * 2 * B * H * T * T * D
 
@@ -51,8 +51,9 @@ def tile_multiqueryattention_pa_t_kernel(tc, x, Wv, bv, q, k, out):
         w_scales = const.tile([P, D], U8, align_bytes=64)
 
         k_sb, q_sb, x_sb = {}, {}, {}
+        k_neg = {}
         kT, x_grouped, x_mx, v_ps, v_grouped, v_mx = {}, {}, {}, {}, {}, {}
-        qT, s_ps, clipped, top, shift, e_sb, rowsum = {}, {}, {}, {}, {}, {}, {}
+        qT, s_ps, clipped, shift, e_sb, rowsum = {}, {}, {}, {}, {}, {}
         eT_ps, e_grouped, e_mx, inverse, o_ps, o_sb = {}, {}, {}, {}, {}, {}
 
         def load_batch(b):
@@ -79,9 +80,22 @@ def tile_multiqueryattention_pa_t_kernel(tc, x, Wv, bv, q, k, out):
                 in_=x[b].rearrange("(u p e) c -> p u (e c)", u=2, p=P, e=2),
             )
 
+        def scale_keys(engine, b, half):
+            if half == 0:
+                k_neg[b] = batch.tile([P, TILES * D], BF16, name="k_neg")
+            columns = slice(half * 2 * D, (half + 1) * 2 * D)
+            engine.tensor_scalar(
+                out=k_neg[b][:, columns],
+                in0=k_sb[b][:, columns],
+                scalar1=-SCALE,
+                scalar2=1.0,
+                op0=ALU.mult,
+                op1=ALU.mult,
+            )
+
         def keys_T(b):
             bank = ps_p.tile([P, BANK], F32, name="bank", tag="prep")
-            transpose_words(bank, k_sb[b][:])
+            transpose_words(bank, k_neg[b][:])
             kT[b] = batch.tile([P, T * 2], BF16, name="kT")
             nc.scalar.copy(out=kT[b][:].bitcast(F32), in_=bank[:])
 
@@ -155,33 +169,29 @@ def tile_multiqueryattention_pa_t_kernel(tc, x, Wv, bv, q, k, out):
                     out=s_ps[j, h][:], lhsT=q_view[:, h, :, e], rhs=k_view[:, :, e], start=(e == 0), stop=(e == 1)
                 )
 
-        def clip_and_max(j, h):
+        def clip_and_min(j, h):
             if h == 0:
                 clipped[j] = work.tile([P, H, T], F32, name="clipped")
-                top[j] = small.tile([P, H], F32, name="top")
+                shift[j] = small.tile([P, H], F32, name="shift")
             nc.vector.tensor_scalar(
                 out=clipped[j][:, h, :],
                 in0=s_ps[j, h][:],
-                scalar1=CLIP_RAW,
-                scalar2=-CLIP_RAW,
-                op0=ALU.min,
-                op1=ALU.max,
-                accum_out=top[j][:, h : h + 1],
+                scalar1=-CLIP,
+                scalar2=CLIP,
+                op0=ALU.max,
+                op1=ALU.min,
+                accum_out=shift[j][:, h : h + 1],
             )
 
-        def lower_clip(j, h):
+        def other_clip(j, h):
             nc.gpsimd.tensor_scalar(
                 out=clipped[j][:, h, :],
                 in0=clipped[j][:, h, :],
-                scalar1=CLIP_RAW,
-                scalar2=-CLIP_RAW,
+                scalar1=CLIP,
+                scalar2=-CLIP,
                 op0=ALU.min,
                 op1=ALU.max,
             )
-
-        def make_shift(j):
-            shift[j] = small.tile([P, H], F32, name="shift")
-            nc.vector.tensor_scalar_mul(out=shift[j][:], in0=top[j][:], scalar1=-SCALE)
 
         def exponential(j, h):
             if h == 0:
@@ -192,7 +202,7 @@ def tile_multiqueryattention_pa_t_kernel(tc, x, Wv, bv, q, k, out):
                 in_=clipped[j][:, h, :],
                 func=ACT.Exp,
                 bias=shift[j][:, h : h + 1],
-                scale=SCALE,
+                scale=-1.0,
                 accum_out=rowsum[j][:, h : h + 1],
             )
 
@@ -241,11 +251,14 @@ def tile_multiqueryattention_pa_t_kernel(tc, x, Wv, bv, q, k, out):
                 o_sb[j] = work.tile([P, H * D], F32, name="o_sb")
             for i in range(2):
                 h = 2 * pair + i
-                nc.vector.tensor_scalar_mul(
-                    out=o_sb[j][:, h * D : (h + 1) * D],
-                    in0=o_ps[j, pair][:, i * D : (i + 1) * D],
-                    scalar1=inverse[j][:, h : h + 1],
-                )
+                o_cols, ps_cols = slice(h * D, (h + 1) * D), slice(i * D, (i + 1) * D)
+                factor = inverse[j][:, h : h + 1]
+                if h < H - 1:
+                    nc.vector.tensor_scalar_mul(out=o_sb[j][:, o_cols], in0=o_ps[j, pair][:, ps_cols], scalar1=factor)
+                else:
+                    nc.scalar.activation(
+                        out=o_sb[j][:, o_cols], in_=o_ps[j, pair][:, ps_cols], func=ACT.Copy, scale=factor
+                    )
 
         def store(j):
             b, t = divmod(j, TILES)
@@ -254,6 +267,8 @@ def tile_multiqueryattention_pa_t_kernel(tc, x, Wv, bv, q, k, out):
         load_batch(0)
         nc.sync.dma_start(out=bias[:], in_=bv.partition_broadcast(P))
         load_batch(1)
+        for half in range(2):
+            scale_keys(nc.vector, 0, half)
         keys_T(0)
         queries_T(0)
         for h in range(H - 1):
@@ -273,14 +288,16 @@ def tile_multiqueryattention_pa_t_kernel(tc, x, Wv, bv, q, k, out):
                 for h in range(H):
                     exponential(j - 1, h)
             if clipping:
-                clip_and_max(j, 0)
-                lower_clip(j, 0)
+                clip_and_min(j, 0)
+                other_clip(j, 0)
             if t == 2 and b + 1 < B:
                 keys_T(b + 1)
                 x_T(b + 1, 0)
             if clipping:
-                clip_and_max(j, 1)
-                lower_clip(j, 1)
+                clip_and_min(j, 1)
+                other_clip(j, 1)
+            if t < 2 and b + 1 < B:
+                scale_keys(nc.gpsimd, b + 1, t)
             if finishing:
                 weighted_values(j - 2, 0)
                 weighted_values(j - 2, 1)
@@ -290,8 +307,8 @@ def tile_multiqueryattention_pa_t_kernel(tc, x, Wv, bv, q, k, out):
                 normalise(j - 2, 0)
             if clipping:
                 for h in range(2, H):
-                    clip_and_max(j, h)
-                    lower_clip(j, h)
+                    clip_and_min(j, h)
+                    other_clip(j, h)
             if j == 0:
                 nc.vector.tensor_copy(out=w_grouped[:], in_=w_raw[:].rearrange("p t d -> p d t"))
             if exponentiating:
@@ -299,8 +316,6 @@ def tile_multiqueryattention_pa_t_kernel(tc, x, Wv, bv, q, k, out):
             if finishing:
                 normalise(j - 2, 1)
                 store(j - 2)
-            if clipping:
-                make_shift(j)
             if exponentiating:
                 e_out(j - 1, 0)
             if t == 2 and b + 1 < B:

@@ -18,7 +18,7 @@ TILES = T // P
 GROUPS = B * TILES
 BANK = 512
 SCALE = 1.0 / 16.0
-CLIP = 100.0
+CLIP_RAW = 100.0 * 16.0
 
 FLOPS = 2 * B * T * C * D + 2 * 2 * B * H * T * T * D
 
@@ -51,9 +51,8 @@ def tile_multiqueryattention_pa_t_kernel(tc, x, Wv, bv, q, k, out):
         w_scales = const.tile([P, D], U8, align_bytes=64)
 
         k_sb, q_sb, x_sb = {}, {}, {}
-        k_neg = {}
         kT, x_grouped, x_mx, v_ps, v_grouped, v_mx = {}, {}, {}, {}, {}, {}
-        qT, s_ps, clipped, shift, e_sb, rowsum = {}, {}, {}, {}, {}, {}
+        qT, s_ps, clipped, top, shift, e_sb, rowsum = {}, {}, {}, {}, {}, {}, {}
         eT_ps, e_grouped, e_mx, inverse, o_ps, o_sb = {}, {}, {}, {}, {}, {}
 
         def load_batch(b):
@@ -80,22 +79,9 @@ def tile_multiqueryattention_pa_t_kernel(tc, x, Wv, bv, q, k, out):
                 in_=x[b].rearrange("(u p e) c -> p u (e c)", u=2, p=P, e=2),
             )
 
-        def scale_keys(engine, b, half):
-            if half == 0:
-                k_neg[b] = batch.tile([P, TILES * D], BF16, name="k_neg")
-            columns = slice(half * 2 * D, (half + 1) * 2 * D)
-            engine.tensor_scalar(
-                out=k_neg[b][:, columns],
-                in0=k_sb[b][:, columns],
-                scalar1=-SCALE,
-                scalar2=1.0,
-                op0=ALU.mult,
-                op1=ALU.mult,
-            )
-
         def keys_T(b):
             bank = ps_p.tile([P, BANK], F32, name="bank", tag="prep")
-            transpose_words(bank, k_neg[b][:])
+            transpose_words(bank, k_sb[b][:])
             kT[b] = batch.tile([P, T * 2], BF16, name="kT")
             nc.scalar.copy(out=kT[b][:].bitcast(F32), in_=bank[:])
 
@@ -169,29 +155,33 @@ def tile_multiqueryattention_pa_t_kernel(tc, x, Wv, bv, q, k, out):
                     out=s_ps[j, h][:], lhsT=q_view[:, h, :, e], rhs=k_view[:, :, e], start=(e == 0), stop=(e == 1)
                 )
 
-        def clip_and_min(j, h):
+        def clip_and_max(j, h):
             if h == 0:
                 clipped[j] = work.tile([P, H, T], F32, name="clipped")
-                shift[j] = small.tile([P, H], F32, name="shift")
+                top[j] = small.tile([P, H], F32, name="top")
             nc.vector.tensor_scalar(
                 out=clipped[j][:, h, :],
                 in0=s_ps[j, h][:],
-                scalar1=-CLIP,
-                scalar2=CLIP,
-                op0=ALU.max,
-                op1=ALU.min,
-                accum_out=shift[j][:, h : h + 1],
+                scalar1=CLIP_RAW,
+                scalar2=-CLIP_RAW,
+                op0=ALU.min,
+                op1=ALU.max,
+                accum_out=top[j][:, h : h + 1],
             )
 
-        def other_clip(j, h):
+        def lower_clip(j, h):
             nc.gpsimd.tensor_scalar(
                 out=clipped[j][:, h, :],
                 in0=clipped[j][:, h, :],
-                scalar1=CLIP,
-                scalar2=-CLIP,
+                scalar1=CLIP_RAW,
+                scalar2=-CLIP_RAW,
                 op0=ALU.min,
                 op1=ALU.max,
             )
+
+        def make_shift(j):
+            shift[j] = small.tile([P, H], F32, name="shift")
+            nc.vector.tensor_scalar_mul(out=shift[j][:], in0=top[j][:], scalar1=-SCALE)
 
         def exponential(j, h):
             if h == 0:
@@ -202,7 +192,7 @@ def tile_multiqueryattention_pa_t_kernel(tc, x, Wv, bv, q, k, out):
                 in_=clipped[j][:, h, :],
                 func=ACT.Exp,
                 bias=shift[j][:, h : h + 1],
-                scale=-1.0,
+                scale=SCALE,
                 accum_out=rowsum[j][:, h : h + 1],
             )
 
@@ -210,21 +200,28 @@ def tile_multiqueryattention_pa_t_kernel(tc, x, Wv, bv, q, k, out):
             eT_ps[j, pair] = ps_a.tile([P, BANK], F32, name="eT_ps", tag="after")
             transpose_words(eT_ps[j, pair], e_sb[j][:, pair * 2 * T : (pair + 1) * 2 * T])
 
-        def e_out(j, pair):
+        def e_out(j, pair, copy=nc.scalar.copy):
             if pair == 0:
                 e_grouped[j] = work.tile([P, H * P * PACK], BF16, name="e_grouped", align_bytes=64)
-            nc.scalar.copy(
+            copy(
                 out=e_grouped[j][:, pair * 2 * BANK : (pair + 1) * 2 * BANK]
                 .bitcast(F32)
                 .rearrange("p (h r u) -> p h r u", h=2, u=2),
                 in_=eT_ps[j, pair][:].rearrange("p (h u r) -> p h r u", h=2, u=2),
             )
 
-        def quantise_e(j):
-            codes = work.tile([P, H * P], U32, name="e_codes", align_bytes=64)
-            scales = work.tile([P, H * P], U8, name="e_scales", align_bytes=64)
-            nc.vector.quantize_mx(out=codes[:].bitcast(FP8X4), scales=scales[:], in_=e_grouped[j][:])
-            e_mx[j] = (codes, scales)
+        def quantise_e(j, heads=slice(0, H)):
+            if heads.start == 0:
+                codes = work.tile([P, H * P], U32, name="e_codes", align_bytes=64)
+                scales = work.tile([P, H * P], U8, name="e_scales", align_bytes=64)
+                e_mx[j] = (codes, scales)
+            codes, scales = e_mx[j]
+            words = slice(heads.start * P, heads.stop * P)
+            nc.vector.quantize_mx(
+                out=codes[:, words].bitcast(FP8X4),
+                scales=scales[:, words],
+                in_=e_grouped[j][:, words.start * PACK : words.stop * PACK],
+            )
 
         def invert(j):
             inverse[j] = small.tile([P, H], F32, name="inverse")
@@ -246,39 +243,39 @@ def tile_multiqueryattention_pa_t_kernel(tc, x, Wv, bv, q, k, out):
                     stop=True,
                 )
 
-        def normalise(j, pair):
+        def normalise(j, pair, scalar=False):
             if pair == 0:
                 o_sb[j] = work.tile([P, H * D], F32, name="o_sb")
             for i in range(2):
                 h = 2 * pair + i
-                o_cols, ps_cols = slice(h * D, (h + 1) * D), slice(i * D, (i + 1) * D)
+                out_cols = o_sb[j][:, h * D : (h + 1) * D]
+                sums = o_ps[j, pair][:, i * D : (i + 1) * D]
                 factor = inverse[j][:, h : h + 1]
-                if h < H - 1:
-                    nc.vector.tensor_scalar_mul(out=o_sb[j][:, o_cols], in0=o_ps[j, pair][:, ps_cols], scalar1=factor)
+                if scalar:
+                    nc.scalar.activation(out=out_cols, in_=sums, func=ACT.Copy, scale=factor)
                 else:
-                    nc.scalar.activation(
-                        out=o_sb[j][:, o_cols], in_=o_ps[j, pair][:, ps_cols], func=ACT.Copy, scale=factor
-                    )
+                    nc.vector.tensor_scalar_mul(out=out_cols, in0=sums, scalar1=factor)
 
-        def store(j):
+        def store(j, heads=slice(0, H)):
             b, t = divmod(j, TILES)
-            nc.sync.dma_start(out=out[b].rearrange("(p t) f -> p t f", t=TILES)[:, t, :], in_=o_sb[j][:])
+            columns = slice(heads.start * D, heads.stop * D)
+            nc.sync.dma_start(
+                out=out[b].rearrange("(p t) f -> p t f", t=TILES)[:, t, columns], in_=o_sb[j][:, columns]
+            )
 
         load_batch(0)
         nc.sync.dma_start(out=bias[:], in_=bv.partition_broadcast(P))
         load_batch(1)
-        for half in range(2):
-            scale_keys(nc.vector, 0, half)
         keys_T(0)
         queries_T(0)
         for h in range(H - 1):
             scores(0, h)
         queries_T(1)
 
-        for j in range(GROUPS + 2):
+        for j in range(GROUPS):
             b, t = divmod(j, TILES)
-            clipping, exponentiating, finishing = j < GROUPS, 1 <= j <= GROUPS, j >= 2
-            projecting = clipping and (t < 2 and b > 0 or j == 1)
+            exponentiating, finishing = j >= 1, j >= 2
+            projecting = t < 2 and b > 0 or j == 1
             half = 0 if j == 1 else t
             if j == 0:
                 x_T(0, 0)
@@ -287,35 +284,31 @@ def tile_multiqueryattention_pa_t_kernel(tc, x, Wv, bv, q, k, out):
             if exponentiating:
                 for h in range(H):
                     exponential(j - 1, h)
-            if clipping:
-                clip_and_min(j, 0)
-                other_clip(j, 0)
-            if t == 2 and b + 1 < B:
+            clip_and_max(j, 0)
+            lower_clip(j, 0)
+            if t == 3 and b + 1 < B:
                 keys_T(b + 1)
+            if t == 2 and b + 1 < B:
                 x_T(b + 1, 0)
-            if clipping:
-                clip_and_min(j, 1)
-                other_clip(j, 1)
-            if t < 2 and b + 1 < B:
-                scale_keys(nc.gpsimd, b + 1, t)
+            clip_and_max(j, 1)
+            lower_clip(j, 1)
             if finishing:
                 weighted_values(j - 2, 0)
                 weighted_values(j - 2, 1)
-            if clipping:
-                scores(j, 3)
+            scores(j, 3)
             if finishing:
                 normalise(j - 2, 0)
-            if clipping:
-                for h in range(2, H):
-                    clip_and_min(j, h)
-                    other_clip(j, h)
+            for h in range(2, H):
+                clip_and_max(j, h)
+                lower_clip(j, h)
             if j == 0:
                 nc.vector.tensor_copy(out=w_grouped[:], in_=w_raw[:].rearrange("p t d -> p d t"))
             if exponentiating:
                 e_T(j - 1, 0)
             if finishing:
-                normalise(j - 2, 1)
+                normalise(j - 2, 1, scalar=projecting)
                 store(j - 2)
+            make_shift(j)
             if exponentiating:
                 e_out(j - 1, 0)
             if t == 2 and b + 1 < B:
@@ -349,3 +342,28 @@ def tile_multiqueryattention_pa_t_kernel(tc, x, Wv, bv, q, k, out):
                 finish_values(0, 1)
             if t == 2 and b + 2 < B:
                 load_batch(b + 2)
+
+        before, last = GROUPS - 2, GROUPS - 1
+        first_heads, other_heads = slice(0, 2), slice(2, H)
+        exponential(last, 0)
+        exponential(last, 1)
+        e_T(last, 0)
+        exponential(last, 2)
+        exponential(last, 3)
+        weighted_values(before, 0)
+        weighted_values(before, 1)
+        e_out(last, 0, nc.vector.tensor_copy)
+        normalise(before, 0)
+        quantise_e(last, first_heads)
+        e_T(last, 1)
+        normalise(before, 1)
+        store(before)
+        invert(last)
+        e_out(last, 1)
+        weighted_values(last, 0)
+        quantise_e(last, other_heads)
+        normalise(last, 0)
+        store(last, first_heads)
+        weighted_values(last, 1)
+        normalise(last, 1)
+        store(last, other_heads)

@@ -163,7 +163,7 @@ def tile_multiqueryattention_pa_t_kernel(tc, x, Wv, bv, q, k, out):
                 out=clipped[j][:, h, :],
                 in0=s_ps[j, h][:],
                 scalar1=CLIP_RAW,
-                scalar2=-CLIP_RAW,
+                scalar2=None,
                 op0=ALU.min,
                 op1=ALU.max,
                 accum_out=top[j][:, h : h + 1],
@@ -181,7 +181,9 @@ def tile_multiqueryattention_pa_t_kernel(tc, x, Wv, bv, q, k, out):
 
         def make_shift(j):
             shift[j] = small.tile([P, H], F32, name="shift")
-            nc.vector.tensor_scalar_mul(out=shift[j][:], in0=top[j][:], scalar1=-SCALE)
+            nc.vector.tensor_scalar(
+                out=shift[j][:], in0=top[j][:], scalar1=-CLIP_RAW, scalar2=-SCALE, op0=ALU.max, op1=ALU.mult
+            )
 
         def exponential(j, h):
             if h == 0:
@@ -301,14 +303,14 @@ def tile_multiqueryattention_pa_t_kernel(tc, x, Wv, bv, q, k, out):
             for h in range(2, H):
                 clip_and_max(j, h)
                 lower_clip(j, h)
-            if j == 0:
-                nc.vector.tensor_copy(out=w_grouped[:], in_=w_raw[:].rearrange("p t d -> p d t"))
             if exponentiating:
                 e_T(j - 1, 0)
             if finishing:
                 normalise(j - 2, 1, scalar=projecting)
                 store(j - 2)
             make_shift(j)
+            if j == 0:
+                nc.vector.tensor_copy(out=w_grouped[:], in_=w_raw[:].rearrange("p t d -> p d t"))
             if exponentiating:
                 e_out(j - 1, 0)
             if t == 2 and b + 1 < B:

from contextlib import ExitStack

import concourse.mybir as mybir
from concourse.masks import make_identity

F32 = mybir.dt.float32
BF16 = mybir.dt.bfloat16
U32 = mybir.dt.uint32
U8 = mybir.dt.uint8
FP8X4 = mybir.dt.float8_e4m3fn_x4
ALU = mybir.AluOpType
ACT = mybir.ActivationFunctionType

B, T, H, D, C = 8, 512, 4, 256, 512
P = 128
PACK = 4
TILES = T // P
GROUPS = B * TILES
BANK = 512
SCALE = 1.0 / 16.0
CLIP_RAW = 100.0 * 16.0

FLOPS = 2 * B * T * C * D + 2 * 2 * B * H * T * T * D


def tile_multiqueryattention_pa_t_kernel(tc, x, Wv, bv, q, k, out):
    nc = tc.nc
    with ExitStack() as ctx:
        const = ctx.enter_context(tc.tile_pool(name="const", bufs=1))
        loads = ctx.enter_context(tc.tile_pool(name="loads", bufs=2))
        batch = ctx.enter_context(tc.tile_pool(name="batch", bufs=2))
        work = ctx.enter_context(tc.tile_pool(name="work", bufs=3))
        small = ctx.enter_context(tc.tile_pool(name="small", bufs=4))
        ps_s = ctx.enter_context(tc.psum_pool(name="ps_s", bufs=3))
        ps_a = ctx.enter_context(tc.psum_pool(name="ps_a", bufs=3))
        ps_p = ctx.enter_context(tc.psum_pool(name="ps_p", bufs=2))
        ctx.enter_context(tc.manual_schedule())

        ident = const.tile([P, P], F32)
        make_identity(nc, ident[:])

        def transpose_words(bank, rows_bf16):
            words = rows_bf16.bitcast(F32)
            for i in range(BANK // P):
                nc.tensor.transpose(bank[:, i * P : (i + 1) * P], words[:, i * P : (i + 1) * P], ident[:])

        w_raw = const.tile([P, PACK, D], BF16)
        bias = const.tile([P, D], BF16)
        w_grouped = const.tile([P, D, PACK], BF16, align_bytes=64)
        w_codes = const.tile([P, D], U32, align_bytes=64)
        w_scales = const.tile([P, D], U8, align_bytes=64)

        k_sb, q_sb, x_sb = {}, {}, {}
        kT, x_grouped, x_mx, v_ps, v_grouped, v_mx = {}, {}, {}, {}, {}, {}
        qT, s_ps, clipped, top, shift, e_sb, rowsum = {}, {}, {}, {}, {}, {}, {}
        eT_ps, e_grouped, e_mx, inverse, o_ps, o_sb = {}, {}, {}, {}, {}, {}

        def load_batch(b):
            k_sb[b] = loads.tile([P, TILES * D], BF16, name="k_sb")
            nc.sync.dma_start(
                out=k_sb[b][:].rearrange("p (a d) -> p a d", a=TILES),
                in_=k[b].rearrange("(a p) d -> p a d", p=P),
            )
            q_sb[b] = loads.tile([P, TILES * H * D], BF16, name="q_sb")
            q_view = q[b].rearrange("(p t) f -> p t f", t=TILES)
            pieces = [slice(0, 1), slice(1, TILES)] if b == 0 else [slice(0, TILES)]
            for tiles in pieces:
                nc.sync.dma_start(
                    out=q_sb[b][:].rearrange("p (t f) -> p t f", t=TILES)[:, tiles, :], in_=q_view[:, tiles, :]
                )
            if b == 0:
                nc.sync.dma_start(
                    out=w_raw[:].rearrange("p (u e) d -> p u (e d)", u=2),
                    in_=Wv.rearrange("(u p e) d -> p u (e d)", u=2, p=P, e=2),
                )
            x_sb[b] = loads.tile([P, TILES * C], BF16, name="x_sb")
            nc.sync.dma_start(
                out=x_sb[b][:].rearrange("p (u f) -> p u f", u=2),
                in_=x[b].rearrange("(u p e) c -> p u (e c)", u=2, p=P, e=2),
            )

        def keys_T(b):
            bank = ps_p.tile([P, BANK], F32, name="bank", tag="prep")
            transpose_words(bank, k_sb[b][:])
            kT[b] = batch.tile([P, T * 2], BF16, name="kT")
            nc.scalar.copy(out=kT[b][:].bitcast(F32), in_=bank[:])

        def queries_T(j):
            b, t = divmod(j, TILES)
            bank = ps_p.tile([P, BANK], F32, name="bank", tag="prep")
            transpose_words(bank, q_sb[b][:, t * H * D : (t + 1) * H * D])
            qT[j] = work.tile([P, H * P * 2], BF16, name="qT")
            nc.scalar.copy(out=qT[j][:].bitcast(F32), in_=bank[:])

        def x_T(b, half):
            if half == 0:
                x_grouped[b] = batch.tile([P, T * PACK], BF16, name="x_grouped", align_bytes=64)
            bank = ps_p.tile([P, BANK], F32, name="bank", tag="prep")
            transpose_words(bank, x_sb[b][:, half * 2 * C : (half + 1) * 2 * C])
            nc.scalar.copy(
                out=x_grouped[b][:, half * 2 * BANK : (half + 1) * 2 * BANK]
                .bitcast(F32)
                .rearrange("p (a r u) -> p a r u", a=2, u=2),
                in_=bank[:].rearrange("p (a u r) -> p a r u", a=2, u=2),
            )

        def quantise_x(b):
            codes = batch.tile([P, T], U32, name="x_codes", align_bytes=64)
            scales = batch.tile([P, T], U8, name="x_scales", align_bytes=64)
            nc.vector.quantize_mx(out=codes[:].bitcast(FP8X4), scales=scales[:], in_=x_grouped[b][:])
            x_mx[b] = (codes, scales)

        def project_values(b, half):
            d_cols = slice(half * P, (half + 1) * P)
            codes, scales = x_mx[b]
            v_ps[b, half] = ps_p.tile([P, BANK], F32, name="v_ps", tag="prep")
            for a in range(TILES):
                rows = slice(a * P, (a + 1) * P)
                nc.tensor.matmul_mx(
                    out=v_ps[b, half][:, rows],
                    lhsT=codes[:, rows].bitcast(FP8X4),
                    lhsT_scale=scales[:, rows],
                    rhs=w_codes[:, d_cols].bitcast(FP8X4),
                    rhs_scale=w_scales[:, d_cols],
                    start=True,
                    stop=True,
                )

        def finish_values(b, half):
            if half == 0:
                v_grouped[b] = batch.tile([P, D, PACK], BF16, name="v_grouped", align_bytes=64)
            d_cols = slice(half * P, (half + 1) * P)
            nc.vector.tensor_tensor(
                out=v_grouped[b][:, d_cols, :],
                in0=v_ps[b, half][:].rearrange("p (a d) -> p d a", a=TILES),
                in1=bias[:, d_cols].unsqueeze(2).to_broadcast([P, P, PACK]),
                op=ALU.add,
            )
            if half == 1:
                v_codes = batch.tile([P, D], U32, name="v_codes", align_bytes=64)
                v_scales = batch.tile([P, D], U8, name="v_scales", align_bytes=64)
                nc.vector.quantize_mx(
                    out=v_codes[:].bitcast(FP8X4),
                    scales=v_scales[:],
                    in_=v_grouped[b][:].rearrange("p d a -> p (d a)"),
                )
                v_mx[b] = (v_codes, v_scales)

        def scores(j, h):
            q_view = qT[j][:].rearrange("p (h r e) -> p h r e", h=H, e=2)
            k_view = kT[j // TILES][:].rearrange("p (r e) -> p r e", e=2)
            s_ps[j, h] = ps_s.tile([P, T], F32, name="s_ps")
            for e in range(2):
                nc.tensor.matmul(
                    out=s_ps[j, h][:], lhsT=q_view[:, h, :, e], rhs=k_view[:, :, e], start=(e == 0), stop=(e == 1)
                )

        def clip_and_max(j, h):
            if h == 0:
                clipped[j] = work.tile([P, H, T], F32, name="clipped")
                top[j] = small.tile([P, H], F32, name="top")
            nc.vector.tensor_scalar(
                out=clipped[j][:, h, :],
                in0=s_ps[j, h][:],
                scalar1=CLIP_RAW,
                scalar2=None,
                op0=ALU.min,
                op1=ALU.max,
                accum_out=top[j][:, h : h + 1],
            )

        def lower_clip(j, h):
            nc.gpsimd.tensor_scalar(
                out=clipped[j][:, h, :],
                in0=clipped[j][:, h, :],
                scalar1=CLIP_RAW,
                scalar2=-CLIP_RAW,
                op0=ALU.min,
                op1=ALU.max,
            )

        def make_shift(j):
            shift[j] = small.tile([P, H], F32, name="shift")
            nc.vector.tensor_scalar(
                out=shift[j][:], in0=top[j][:], scalar1=-CLIP_RAW, scalar2=-SCALE, op0=ALU.max, op1=ALU.mult
            )

        def exponential(j, h):
            if h == 0:
                e_sb[j] = work.tile([P, H * T], BF16, name="e_sb")
                rowsum[j] = small.tile([P, H], F32, name="rowsum")
            nc.scalar.activation(
                out=e_sb[j][:, h * T : (h + 1) * T],
                in_=clipped[j][:, h, :],
                func=ACT.Exp,
                bias=shift[j][:, h : h + 1],
                scale=SCALE,
                accum_out=rowsum[j][:, h : h + 1],
            )

        def e_T(j, pair):
            eT_ps[j, pair] = ps_a.tile([P, BANK], F32, name="eT_ps", tag="after")
            transpose_words(eT_ps[j, pair], e_sb[j][:, pair * 2 * T : (pair + 1) * 2 * T])

        def e_out(j, pair, copy=nc.scalar.copy):
            if pair == 0:
                e_grouped[j] = work.tile([P, H * P * PACK], BF16, name="e_grouped", align_bytes=64)
            copy(
                out=e_grouped[j][:, pair * 2 * BANK : (pair + 1) * 2 * BANK]
                .bitcast(F32)
                .rearrange("p (h r u) -> p h r u", h=2, u=2),
                in_=eT_ps[j, pair][:].rearrange("p (h u r) -> p h r u", h=2, u=2),
            )

        def quantise_e(j, heads=slice(0, H)):
            if heads.start == 0:
                codes = work.tile([P, H * P], U32, name="e_codes", align_bytes=64)
                scales = work.tile([P, H * P], U8, name="e_scales", align_bytes=64)
                e_mx[j] = (codes, scales)
            codes, scales = e_mx[j]
            words = slice(heads.start * P, heads.stop * P)
            nc.vector.quantize_mx(
                out=codes[:, words].bitcast(FP8X4),
                scales=scales[:, words],
                in_=e_grouped[j][:, words.start * PACK : words.stop * PACK],
            )

        def invert(j):
            inverse[j] = small.tile([P, H], F32, name="inverse")
            nc.vector.reciprocal(out=inverse[j][:], in_=rowsum[j][:])

        def weighted_values(j, pair):
            codes, scales = e_mx[j]
            v_codes, v_scales = v_mx[j // TILES]
            o_ps[j, pair] = ps_a.tile([P, BANK], F32, name="o_ps", tag="after")
            for i in range(2):
                rows = slice((2 * pair + i) * P, (2 * pair + i + 1) * P)
                nc.tensor.matmul_mx(
                    out=o_ps[j, pair][:, i * D : (i + 1) * D],
                    lhsT=codes[:, rows].bitcast(FP8X4),
                    lhsT_scale=scales[:, rows],
                    rhs=v_codes[:].bitcast(FP8X4),
                    rhs_scale=v_scales[:],
                    start=True,
                    stop=True,
                )

        def normalise(j, pair, scalar=False):
            if pair == 0:
                o_sb[j] = work.tile([P, H * D], F32, name="o_sb")
            for i in range(2):
                h = 2 * pair + i
                out_cols = o_sb[j][:, h * D : (h + 1) * D]
                sums = o_ps[j, pair][:, i * D : (i + 1) * D]
                factor = inverse[j][:, h : h + 1]
                if scalar:
                    nc.scalar.activation(out=out_cols, in_=sums, func=ACT.Copy, scale=factor)
                else:
                    nc.vector.tensor_scalar_mul(out=out_cols, in0=sums, scalar1=factor)

        def store(j, heads=slice(0, H)):
            b, t = divmod(j, TILES)
            columns = slice(heads.start * D, heads.stop * D)
            nc.sync.dma_start(
                out=out[b].rearrange("(p t) f -> p t f", t=TILES)[:, t, columns], in_=o_sb[j][:, columns]
            )

        load_batch(0)
        nc.sync.dma_start(out=bias[:], in_=bv.partition_broadcast(P))
        load_batch(1)
        keys_T(0)
        queries_T(0)
        for h in range(H - 1):
            scores(0, h)
        queries_T(1)

        for j in range(GROUPS):
            b, t = divmod(j, TILES)
            exponentiating, finishing = j >= 1, j >= 2
            projecting = t < 2 and b > 0 or j == 1
            half = 0 if j == 1 else t
            if j == 0:
                x_T(0, 0)
            if projecting:
                project_values(b, half)
            if exponentiating:
                for h in range(H):
                    exponential(j - 1, h)
            clip_and_max(j, 0)
            lower_clip(j, 0)
            if t == 3 and b + 1 < B:
                keys_T(b + 1)
            if t == 2 and b + 1 < B:
                x_T(b + 1, 0)
            clip_and_max(j, 1)
            lower_clip(j, 1)
            if finishing:
                weighted_values(j - 2, 0)
                weighted_values(j - 2, 1)
            scores(j, 3)
            if finishing:
                normalise(j - 2, 0)
            for h in range(2, H):
                clip_and_max(j, h)
                lower_clip(j, h)
            if exponentiating:
                e_T(j - 1, 0)
            if finishing:
                normalise(j - 2, 1, scalar=projecting)
                store(j - 2)
            make_shift(j)
            if j == 0:
                nc.vector.tensor_copy(out=w_grouped[:], in_=w_raw[:].rearrange("p t d -> p d t"))
            if exponentiating:
                e_out(j - 1, 0)
            if t == 2 and b + 1 < B:
                x_T(b + 1, 1)
                quantise_x(b + 1)
            if exponentiating:
                e_T(j - 1, 1)
                invert(j - 1)
            if projecting:
                finish_values(b, half)
            if exponentiating:
                e_out(j - 1, 1)
            if j == 0:
                x_T(0, 1)
                nc.vector.quantize_mx(
                    out=w_codes[:].bitcast(FP8X4),
                    scales=w_scales[:],
                    in_=w_grouped[:].rearrange("p d t -> p (d t)"),
                )
                quantise_x(0)
            if j + 2 < GROUPS:
                queries_T(j + 2)
            if j == 1:
                project_values(0, 1)
            if j + 1 < GROUPS:
                for h in range(H - 1):
                    scores(j + 1, h)
            if exponentiating:
                quantise_e(j - 1)
            if j == 1:
                finish_values(0, 1)
            if t == 2 and b + 2 < B:
                load_batch(b + 2)

        before, last = GROUPS - 2, GROUPS - 1
        first_heads, other_heads = slice(0, 2), slice(2, H)
        exponential(last, 0)
        exponential(last, 1)
        e_T(last, 0)
        exponential(last, 2)
        exponential(last, 3)
        weighted_values(before, 0)
        weighted_values(before, 1)
        e_out(last, 0, nc.vector.tensor_copy)
        normalise(before, 0)
        quantise_e(last, first_heads)
        e_T(last, 1)
        normalise(before, 1)
        store(before)
        invert(last)
        e_out(last, 1)
        weighted_values(last, 0)
        quantise_e(last, other_heads)
        normalise(last, 0)
        store(last, first_heads)
        weighted_values(last, 1)
        normalise(last, 1)
        store(last, other_heads)
